import numpy as np
import ml_dtypes


def mxq(x, axis, fmt="e4m3"):
    dtype, down = {"e4m3": (ml_dtypes.float8_e4m3fn, 7), "e5m2": (ml_dtypes.float8_e5m2, 14)}[fmt]
    v = np.moveaxis(np.asarray(x, np.float32).astype(ml_dtypes.bfloat16).astype(np.float64), axis, -1)
    blocks = v.reshape(v.shape[:-1] + (-1, 32))
    amax = np.abs(blocks).max(-1, keepdims=True)
    byte = np.maximum(np.where(amax > 0, np.frexp(amax)[1] - 1 + 127, 0) - down, 1)
    scale = np.exp2(byte - 127.0)
    codes = (blocks / scale).astype(np.float32).astype(dtype).astype(np.float64)
    return np.moveaxis((codes * scale).reshape(v.shape), -1, axis)


WIDE = False


def mx_kscale(k):
    if not WIDE:
        return np.ones(k)
    levels = np.array([10, -10, 5, -5, 0])
    if k % 512:
        return np.exp2(np.random.permutation(np.resize(levels, k // 32))).repeat(32)
    a = np.empty((k // 512, 16))
    for p in range(k // 512):
        a[p, :8] = np.random.permutation(np.resize(levels, 8))
        for g in range(8):
            far = levels[np.abs(levels - a[p, g]) >= 10]
            a[p, g + 8] = far[np.random.randint(len(far))]
    return np.exp2(a.ravel()).repeat(32)


BF16 = ml_dtypes.bfloat16


def bf(x):
    return np.asarray(x, np.float32).astype(BF16)


def f64(x):
    return np.asarray(x).astype(np.float64)


B, D, MID, NH = 512, 2048, 2048, 4
HALF = D // 2


def setup_inputs():
    s, t = mx_kscale(MID), mx_kscale(MID)
    return {"h": bf(np.maximum(np.random.standard_normal((B, MID)), 0.0) * s),
            "x": bf(np.random.standard_normal((B, D))),
            "w_h": bf(np.random.standard_normal((MID, MID)) * np.sqrt(2.0 / MID) / s[:, None] * t),
            "b_h": bf(np.random.standard_normal(MID) * 0.3 * t),
            "w_out": bf(np.random.standard_normal((MID, HALF)) * np.sqrt(2.0 / MID) / t[:, None]),
            "b_out": bf(np.random.standard_normal(HALF) * 0.3)}


def reference(h, x, w_h, b_h, w_out, b_out):
    xr = f64(x).reshape(B, HALF, 2)
    x1, x2 = xr[:, :, 0], xr[:, :, 1]
    g = np.maximum((mxq(f64(h), 1, "e4m3") @ mxq(f64(w_h), 0, "e4m3")) + f64(b_h), 0.0)
    shift = (mxq(g, 1, "e4m3") @ mxq(f64(w_out), 0, "e4m3")) + f64(b_out)
    return np.stack((x1 + shift, x2), axis=2).reshape(B, D)

@@ -1,0 +1,318 @@
+from contextlib import ExitStack
+
+import concourse.mybir as mybir
+from concourse.masks import make_identity
+
+F32 = mybir.dt.float32
+BF16 = mybir.dt.bfloat16
+U32 = mybir.dt.uint32
+U8 = mybir.dt.uint8
+FP8X4 = mybir.dt.float8_e4m3fn_x4
+ACT = mybir.ActivationFunctionType
+ALU = mybir.AluOpType
+
+P = 128
+B = 512
+MID = 2048
+HALF = 1024
+FLOPS = 2 * B * MID * MID + 2 * B * MID * HALF
+
+WH_V_COLS_FIRST = 600
+WH_V_COLS = 576
+WH_V_COLS_LATE = 608
+WO_V_PASSES = (2, 2, 2, 1)
+RAW_BUFS = 6
+
+
+def regroup(engine_copy, dst, src):
+    engine_copy(
+        out=dst.rearrange("p (c i t) -> p c t i", i=4, t=4),
+        in_=src.rearrange("p t (c i) -> p c t i", i=4),
+    )
+
+
+def regroup_wh_columns(engine_copy, dst, src, lo, hi):
+    engine_copy(
+        out=dst.rearrange("p (t c j) -> p c j t", t=4, j=4)[:, lo:hi],
+        in_=src.rearrange("p j (c t) -> p c j t", t=4)[:, lo:hi],
+    )
+
+
+def tile_additivecoupling_pa_kernel(tc, h, x, w_h, b_h, w_out, b_out, out):
+    nc = tc.nc
+    with ExitStack() as ctx:
+        const = ctx.enter_context(tc.tile_pool(name="const", bufs=1))
+        keep = ctx.enter_context(tc.tile_pool(name="keep", bufs=1))
+        act = ctx.enter_context(tc.tile_pool(name="act", bufs=4))
+        rawp = ctx.enter_context(tc.tile_pool(name="rawp", bufs=RAW_BUFS))
+        stagep = ctx.enter_context(tc.tile_pool(name="stagep", bufs=3))
+        grp = ctx.enter_context(tc.tile_pool(name="grp", bufs=4))
+        gpp = ctx.enter_context(tc.tile_pool(name="gpp", bufs=2))
+        outp = ctx.enter_context(tc.tile_pool(name="outp", bufs=6))
+        ps = ctx.enter_context(tc.psum_pool(name="ps", bufs=8))
+
+        h_codes = keep.tile([P, 4, B], U32, name="h_codes", align_bytes=64)
+        h_scales = keep.tile([P, 4, B], U8, name="h_scales", align_bytes=64)
+        wh_codes = keep.tile([P, 4, MID], U32, name="wh_codes", align_bytes=64)
+        wh_scales = keep.tile([P, 4, MID], U8, name="wh_scales", align_bytes=64)
+        g_codes = keep.tile([P, 4, B], U32, name="g_codes", align_bytes=64)
+        g_scales = keep.tile([P, 4, B], U8, name="g_scales", align_bytes=64)
+        wo_codes = keep.tile([P, 4, HALF], U32, name="wo_codes", align_bytes=64)
+        wo_scales = keep.tile([P, 4, HALF], U8, name="wo_scales", align_bytes=64)
+
+        raw = {}
+        stage = {}
+        accs = {}
+        gp = {}
+        gg = {}
+        x_sb = []
+        h_sb = []
+
+        def load_raw(i):
+            if i >= 12:
+                return
+            t = rawp.tile([P, 4, HALF], BF16, name="raw%d" % i, tag="raw")
+            raw[i] = t
+            if i < 8:
+                hh, c = divmod(i, 4)
+                src = w_h[512 * c : 512 * c + 512, HALF * hh : HALF * hh + HALF]
+                nc.sync.dma_start(out=t[:], in_=src.rearrange("(p j) w -> p j w", j=4))
+            else:
+                jh, gp2 = divmod(i - 8, 2)
+                src = w_out[1024 * gp2 : 1024 * gp2 + 1024, 512 * jh : 512 * jh + 512]
+                for g2 in range(2):
+                    nc.sync.dma_start(
+                        out=t[:].rearrange("p a (b n) -> p (a b) n", b=2)[:, 4 * g2 : 4 * g2 + 4, :],
+                        in_=src[512 * g2 : 512 * g2 + 512, :].rearrange("(p t) n -> p t n", t=4),
+                    )
+
+        def regroup_wh(i):
+            vc = WH_V_COLS_FIRST if i < 2 else (WH_V_COLS if i < 5 else WH_V_COLS_LATE)
+            st = stagep.tile([P, 4 * HALF], BF16, name="st%d" % i, tag="stage", align_bytes=64)
+            stage[i] = st
+            regroup_wh_columns(nc.vector.tensor_copy, st[:], raw[i][:], 0, vc // 4)
+            regroup_wh_columns(nc.scalar.copy, st[:], raw[i][:], vc // 4, 256)
+
+        def quantise_wh(i):
+            hh, c = divmod(i, 4)
+            cols = slice(HALF * hh, HALF * hh + HALF)
+            nc.vector.quantize_mx(
+                out=wh_codes[:, c, cols].bitcast(FP8X4), scales=wh_scales[:, c, cols], in_=stage[i][:]
+            )
+            load_raw(i + RAW_BUFS)
+
+        def matmul1(i):
+            hh, c = divmod(i, 4)
+            for m8 in range(8):
+                m = 8 * hh + m8
+                if c == 0:
+                    accs[m] = ps.tile([P, 512], F32, name="acc%d" % m, tag="bank")
+                col = HALF * hh + 256 * (m8 % 4) + P * (m8 // 4)
+                mc = slice(col, col + P)
+                nc.tensor.matmul_mx(
+                    out=accs[m][:],
+                    lhsT=wh_codes[:, c, mc].bitcast(FP8X4),
+                    lhsT_scale=wh_scales[:, c, mc],
+                    rhs=h_codes[:, c, :].bitcast(FP8X4),
+                    rhs_scale=h_scales[:, c, :],
+                    start=(c == 0),
+                    stop=(c == 3),
+                )
+
+        def drain_g(m, on_vector):
+            g, t4 = divmod(m, 4)
+            if t4 == 0:
+                gp[g] = gpp.tile([P, 4, B], BF16, name="gp%d" % g, tag="gp")
+            if on_vector:
+                nc.vector.tensor_scalar(
+                    out=gp[g][:, t4, :],
+                    in0=accs[m][:],
+                    scalar1=bias[:, m : m + 1],
+                    scalar2=0.0,
+                    op0=ALU.add,
+                    op1=ALU.max,
+                )
+            else:
+                nc.scalar.activation(
+                    out=gp[g][:, t4, :], in_=accs[m][:], func=ACT.Relu, bias=bias[:, m : m + 1], scale=1.0
+                )
+
+        def regroup_g(g):
+            gg[g] = grp.tile([P, 4 * B], BF16, name="gg%d" % g, tag="grp", align_bytes=64)
+            regroup(nc.vector.tensor_copy, gg[g][:], gp[g][:])
+
+        def quantise_g(g):
+            nc.vector.quantize_mx(
+                out=g_codes[:, g, :].bitcast(FP8X4), scales=g_scales[:, g, :], in_=gg[g][:]
+            )
+
+        def regroup_wo(q):
+            st = stagep.tile([P, 4 * HALF], BF16, name="sq%d" % q, tag="stage", align_bytes=64)
+            stage[8 + q] = st
+            for g in range(4):
+                eng = nc.vector.tensor_copy if g < WO_V_PASSES[q] else nc.scalar.copy
+                piece = raw[8 + 2 * (q // 2) + g // 2][:].rearrange("p a (b n) -> p (a b) n", b=2)
+                rows = slice(4 * (g % 2), 4 * (g % 2) + 4)
+                cols = slice(256 * (q % 2), 256 * (q % 2) + 256)
+                regroup(eng, st[:, HALF * g : HALF * g + HALF], piece[:, rows, cols])
+
+        def quantise_wo(q):
+            nc.vector.quantize_mx(
+                out=wo_codes[:, q, :].bitcast(FP8X4), scales=wo_scales[:, q, :], in_=stage[8 + q][:]
+            )
+
+        banks = {}
+
+        def x_plus_bias(q):
+            for hb in range(2):
+                xb = ps.tile([P, 512], F32, name="xb%d_%d" % (q, hb), tag="bank")
+                for k in range(2):
+                    cols = slice(256 * k, 256 * k + 256)
+                    nc.tensor.matmul(
+                        out=xb[:, cols],
+                        lhsT=ident_bf[:],
+                        rhs=x_sb[2 * hb + k][:].rearrange("p (j e) -> p e j", e=2)[:, 0, 256 * q : 256 * q + 256],
+                        start=True,
+                        stop=False,
+                    )
+                    nc.tensor.matmul(
+                        out=xb[:, cols],
+                        lhsT=ones_bf[:],
+                        rhs=brow[:, 256 * q : 256 * q + 256],
+                        start=False,
+                        stop=True,
+                    )
+                nc.scalar.copy(out=tplane[q % 2][:, 0, 512 * hb : 512 * hb + 512], in_=xb[:])
+
+        def matmul2(q, bt):
+            bank = ps.tile([P, 512], F32, name="sh%d_%d" % (q, bt), tag="bank")
+            banks[bt] = bank
+            nc.tensor.matmul(
+                out=bank[:, 256:512],
+                lhsT=ident_bf[:],
+                rhs=x_sb[bt][:].rearrange("p (j e) -> p e j", e=2)[:, 1, 256 * q : 256 * q + 256],
+                start=True,
+                stop=True,
+            )
+            for g in range(4):
+                nc.tensor.matmul_mx(
+                    out=bank[:, 0:256],
+                    lhsT=g_codes[:, g, P * bt : P * bt + P].bitcast(FP8X4),
+                    lhsT_scale=g_scales[:, g, P * bt : P * bt + P],
+                    rhs=wo_codes[:, q, 256 * g : 256 * g + 256].bitcast(FP8X4),
+                    rhs_scale=wo_scales[:, q, 256 * g : 256 * g + 256],
+                    start=(g == 0),
+                    stop=(g == 3),
+                )
+
+        def add_and_store(q, bt):
+            o = outp.tile([P, 512], F32, name="o%d_%d" % (q, bt), tag="o")
+            nc.vector.tensor_tensor(
+                out=o[:].rearrange("p (j e) -> p j e", e=2),
+                in0=banks[bt][:].rearrange("p (e j) -> p j e", e=2),
+                in1=tplane[q % 2][:, :, 256 * bt : 256 * bt + 256].rearrange("p e j -> p j e"),
+                op=ALU.add,
+            )
+            nc.sync.dma_start(out=out[P * bt : P * bt + P, 512 * q : 512 * q + 512], in_=o[:])
+
+        load_raw(0)
+        load_raw(1)
+        for bt in range(4):
+            t = act.tile([P, MID], BF16, name="h%d" % bt, tag="act")
+            nc.sync.dma_start(out=t[:], in_=h[P * bt : P * bt + P, :])
+            h_sb.append(t)
+        for i in range(2, RAW_BUFS):
+            load_raw(i)
+
+        ident = const.tile([P, P], F32, name="ident")
+        make_identity(nc, ident[:])
+        ident_bf = const.tile([P, P], BF16, name="ident_bf")
+        make_identity(nc, ident_bf[:])
+        ones_bf = const.tile([P, P], BF16, name="ones_bf")
+        nc.vector.memset(ones_bf[:], 1.0)
+        brow = const.tile([P, HALF], BF16, name="brow")
+        nc.vector.memset(brow[:], 0.0)
+        nc.scalar.dma_start(out=brow[0:1, :], in_=b_out.rearrange("(o n) -> o n", o=1))
+        tplane = []
+        for k in range(2):
+            tpl = const.tile([P, 2, HALF], F32, name="tplane%d" % k)
+            nc.vector.memset(tpl[:, 1, :], 0.0)
+            tplane.append(tpl)
+        bias = const.tile([P, 16], BF16, name="bias")
+        nc.scalar.dma_start(
+            out=bias[:].rearrange("p (g t) -> p g t", t=4), in_=b_h.rearrange("(g p t) -> p g t", p=P, t=4)
+        )
+
+        regroup_wh(0)
+        quantise_wh(0)
+        regroup_wh(1)
+        quantise_wh(1)
+
+        gh = []
+        for c in range(4):
+            gh.append(grp.tile([P, 4 * B], BF16, name="gh%d" % c, tag="grp", align_bytes=64))
+        for bh in range(2):
+            for c in range(4):
+                tp = ps.tile([P, 512], F32, name="tp%d_%d" % (bh, c), tag="bank")
+                for u in range(2):
+                    for b2 in range(2):
+                        words = h_sb[2 * bh + b2][:].bitcast(F32).rearrange(
+                            "p (c q u) -> p c u q", c=4, u=2
+                        )
+                        nc.tensor.transpose(
+                            out=tp[:, 256 * u + P * b2 : 256 * u + P * b2 + P],
+                            in_=words[:, c, u, :],
+                            identity=ident[:],
+                        )
+                dst = gh[c][:].bitcast(F32).rearrange("p (b u) -> p b u", u=2)
+                nc.scalar.copy(
+                    out=dst[:, 256 * bh : 256 * bh + 256, :], in_=tp[:].rearrange("p (u b) -> p b u", u=2)
+                )
+        for c in range(4):
+            nc.vector.quantize_mx(
+                out=h_codes[:, c, :].bitcast(FP8X4), scales=h_scales[:, c, :], in_=gh[c][:]
+            )
+        matmul1(0)
+        matmul1(1)
+
+        regroup_wh(2)
+        for i in range(2, 8):
+            if i + 1 < 8:
+                regroup_wh(i + 1)
+            quantise_wh(i)
+            if i == 3:
+                for bt in range(4):
+                    t = act.tile([P, MID], BF16, name="x%d" % bt, tag="act")
+                    nc.sync.dma_start(out=t[:], in_=x[P * bt : P * bt + P, :])
+                    x_sb.append(t)
+            matmul1(i)
+            if i == 4:
+                for m in range(8):
+                    drain_g(m, False)
+            if i == 5:
+                regroup_g(0)
+                quantise_g(0)
+            if i == 6:
+                regroup_g(1)
+                quantise_g(1)
+        regroup_wo(0)
+        quantise_wo(0)
+        for m in range(8, 16):
+            drain_g(m, m in (9, 11))
+            if m == 11:
+                regroup_g(2)
+        quantise_g(2)
+        regroup_g(3)
+        quantise_g(3)
+        regroup_wo(1)
+        quantise_wo(1)
+
+        for q in range(4):
+            x_plus_bias(q)
+            for bt in range(4):
+                matmul2(q, bt)
+            if q + 2 < 4:
+                regroup_wo(q + 2)
+                quantise_wo(q + 2)
+            for bt in range(4):
+                add_and_store(q, bt)

@@ -208,9 +208,9 @@ def tile_additivecoupling_pa_kernel(tc, h, x, w_h, b_h, w_out, b_out, out):
         def add_and_store(q, bt):
             o = outp.tile([P, 512], F32, name="o%d_%d" % (q, bt), tag="o")
             nc.vector.tensor_tensor(
-                out=o[:].rearrange("p (j e) -> p j e", e=2),
-                in0=banks[bt][:].rearrange("p (e j) -> p j e", e=2),
-                in1=tplane[q % 2][:, :, 256 * bt : 256 * bt + 256].rearrange("p e j -> p j e"),
+                out=o[:].rearrange("p (k i e) -> p k e i", i=2, e=2),
+                in0=banks[bt][:].rearrange("p (e k i) -> p k e i", e=2, i=2),
+                in1=tplane[q % 2][:, :, 256 * bt : 256 * bt + 256].rearrange("p e (k i) -> p k e i", i=2),
                 op=ALU.add,
             )
             nc.sync.dma_start(out=out[P * bt : P * bt + P, 512 * q : 512 * q + 512], in_=o[:])

@@ -184,19 +184,22 @@ def tile_additivecoupling_pa_kernel(tc, h, x, w_h, b_h, w_out, b_out, out):
                     )
                 nc.scalar.copy(out=tplane[q % 2][:, 0, 512 * hb : 512 * hb + 512], in_=xb[:])
 
+        def x_odd(u):
+            q = u // 2
+            for bt in (2 * (u % 2), 2 * (u % 2) + 1):
+                banks[(q, bt)] = ps.tile([P, 512], F32, name="sh%d_%d" % (q, bt), tag="bank")
+                nc.tensor.matmul(
+                    out=banks[(q, bt)][:, 256:512],
+                    lhsT=ident_bf[:],
+                    rhs=x_sb[bt][:].rearrange("p (j e) -> p e j", e=2)[:, 1, 256 * q : 256 * q + 256],
+                    start=True,
+                    stop=True,
+                )
+
         def matmul2(q, bt):
-            bank = ps.tile([P, 512], F32, name="sh%d_%d" % (q, bt), tag="bank")
-            banks[bt] = bank
-            nc.tensor.matmul(
-                out=bank[:, 256:512],
-                lhsT=ident_bf[:],
-                rhs=x_sb[bt][:].rearrange("p (j e) -> p e j", e=2)[:, 1, 256 * q : 256 * q + 256],
-                start=True,
-                stop=True,
-            )
             for g in range(4):
                 nc.tensor.matmul_mx(
-                    out=bank[:, 0:256],
+                    out=banks[(q, bt)][:, 0:256],
                     lhsT=g_codes[:, g, P * bt : P * bt + P].bitcast(FP8X4),
                     lhsT_scale=g_scales[:, g, P * bt : P * bt + P],
                     rhs=wo_codes[:, q, 256 * g : 256 * g + 256].bitcast(FP8X4),
@@ -209,11 +212,15 @@ def tile_additivecoupling_pa_kernel(tc, h, x, w_h, b_h, w_out, b_out, out):
             o = outp.tile([P, 512], F32, name="o%d_%d" % (q, bt), tag="o")
             nc.vector.tensor_tensor(
                 out=o[:].rearrange("p (k i e) -> p k e i", i=2, e=2),
-                in0=banks[bt][:].rearrange("p (e k i) -> p k e i", e=2, i=2),
+                in0=banks[(q, bt)][:].rearrange("p (e k i) -> p k e i", e=2, i=2),
                 in1=tplane[q % 2][:, :, 256 * bt : 256 * bt + 256].rearrange("p e (k i) -> p k e i", i=2),
                 op=ALU.add,
             )
             nc.sync.dma_start(out=out[P * bt : P * bt + P, 512 * q : 512 * q + 512], in_=o[:])
+
+        warm = const.tile([P, 2], F32, name="warm")
+        nc.vector.memset(warm[:, 0:1], 0.0)
+        nc.scalar.activation(out=warm[:, 1:2], in_=warm[:, 0:1], func=ACT.Relu)
 
         load_raw(0)
         load_raw(1)
@@ -307,12 +314,22 @@ def tile_additivecoupling_pa_kernel(tc, h, x, w_h, b_h, w_out, b_out, out):
         regroup_wo(1)
         quantise_wo(1)
 
-        for q in range(4):
-            x_plus_bias(q)
-            for bt in range(4):
+        x_plus_bias(0)
+        x_odd(0)
+        x_odd(1)
+        for u in range(8):
+            q, second = divmod(u, 2)
+            pair = (2 * second, 2 * second + 1)
+            for bt in pair:
                 matmul2(q, bt)
+            if second == 0 and q + 1 < 4:
+                x_plus_bias(q + 1)
+            if u + 2 < 8:
+                x_odd(u + 2)
             if q + 2 < 4:
-                regroup_wo(q + 2)
-                quantise_wo(q + 2)
-            for bt in range(4):
+                if second == 0:
+                    regroup_wo(q + 2)
+                else:
+                    quantise_wo(q + 2)
+            for bt in pair:
                 add_and_store(q, bt)

from contextlib import ExitStack

import concourse.mybir as mybir
from concourse.masks import make_identity

F32 = mybir.dt.float32
BF16 = mybir.dt.bfloat16
U32 = mybir.dt.uint32
U8 = mybir.dt.uint8
FP8X4 = mybir.dt.float8_e4m3fn_x4
ACT = mybir.ActivationFunctionType
ALU = mybir.AluOpType

P = 128
B = 512
MID = 2048
HALF = 1024
FLOPS = 2 * B * MID * MID + 2 * B * MID * HALF

WH_V_COLS_FIRST = 600
WH_V_COLS = 576
WH_V_COLS_LATE = 608
WO_V_PASSES = (2, 2, 2, 1)
RAW_BUFS = 6


def regroup(engine_copy, dst, src):
    engine_copy(
        out=dst.rearrange("p (c i t) -> p c t i", i=4, t=4),
        in_=src.rearrange("p t (c i) -> p c t i", i=4),
    )


def regroup_wh_columns(engine_copy, dst, src, lo, hi):
    engine_copy(
        out=dst.rearrange("p (t c j) -> p c j t", t=4, j=4)[:, lo:hi],
        in_=src.rearrange("p j (c t) -> p c j t", t=4)[:, lo:hi],
    )


def tile_additivecoupling_pa_kernel(tc, h, x, w_h, b_h, w_out, b_out, out):
    nc = tc.nc
    with ExitStack() as ctx:
        const = ctx.enter_context(tc.tile_pool(name="const", bufs=1))
        keep = ctx.enter_context(tc.tile_pool(name="keep", bufs=1))
        act = ctx.enter_context(tc.tile_pool(name="act", bufs=4))
        rawp = ctx.enter_context(tc.tile_pool(name="rawp", bufs=RAW_BUFS))
        stagep = ctx.enter_context(tc.tile_pool(name="stagep", bufs=3))
        grp = ctx.enter_context(tc.tile_pool(name="grp", bufs=4))
        gpp = ctx.enter_context(tc.tile_pool(name="gpp", bufs=2))
        outp = ctx.enter_context(tc.tile_pool(name="outp", bufs=6))
        ps = ctx.enter_context(tc.psum_pool(name="ps", bufs=8))

        h_codes = keep.tile([P, 4, B], U32, name="h_codes", align_bytes=64)
        h_scales = keep.tile([P, 4, B], U8, name="h_scales", align_bytes=64)
        wh_codes = keep.tile([P, 4, MID], U32, name="wh_codes", align_bytes=64)
        wh_scales = keep.tile([P, 4, MID], U8, name="wh_scales", align_bytes=64)
        g_codes = keep.tile([P, 4, B], U32, name="g_codes", align_bytes=64)
        g_scales = keep.tile([P, 4, B], U8, name="g_scales", align_bytes=64)
        wo_codes = keep.tile([P, 4, HALF], U32, name="wo_codes", align_bytes=64)
        wo_scales = keep.tile([P, 4, HALF], U8, name="wo_scales", align_bytes=64)

        raw = {}
        stage = {}
        accs = {}
        gp = {}
        gg = {}
        x_sb = []
        h_sb = []

        def load_raw(i):
            if i >= 12:
                return
            t = rawp.tile([P, 4, HALF], BF16, name="raw%d" % i, tag="raw")
            raw[i] = t
            if i < 8:
                hh, c = divmod(i, 4)
                src = w_h[512 * c : 512 * c + 512, HALF * hh : HALF * hh + HALF]
                nc.sync.dma_start(out=t[:], in_=src.rearrange("(p j) w -> p j w", j=4))
            else:
                jh, gp2 = divmod(i - 8, 2)
                src = w_out[1024 * gp2 : 1024 * gp2 + 1024, 512 * jh : 512 * jh + 512]
                for g2 in range(2):
                    nc.sync.dma_start(
                        out=t[:].rearrange("p a (b n) -> p (a b) n", b=2)[:, 4 * g2 : 4 * g2 + 4, :],
                        in_=src[512 * g2 : 512 * g2 + 512, :].rearrange("(p t) n -> p t n", t=4),
                    )

        def regroup_wh(i):
            vc = WH_V_COLS_FIRST if i < 2 else (WH_V_COLS if i < 5 else WH_V_COLS_LATE)
            st = stagep.tile([P, 4 * HALF], BF16, name="st%d" % i, tag="stage", align_bytes=64)
            stage[i] = st
            regroup_wh_columns(nc.vector.tensor_copy, st[:], raw[i][:], 0, vc // 4)
            regroup_wh_columns(nc.scalar.copy, st[:], raw[i][:], vc // 4, 256)

        def quantise_wh(i):
            hh, c = divmod(i, 4)
            cols = slice(HALF * hh, HALF * hh + HALF)
            nc.vector.quantize_mx(
                out=wh_codes[:, c, cols].bitcast(FP8X4), scales=wh_scales[:, c, cols], in_=stage[i][:]
            )
            load_raw(i + RAW_BUFS)

        def matmul1(i):
            hh, c = divmod(i, 4)
            for m8 in range(8):
                m = 8 * hh + m8
                if c == 0:
                    accs[m] = ps.tile([P, 512], F32, name="acc%d" % m, tag="bank")
                col = HALF * hh + 256 * (m8 % 4) + P * (m8 // 4)
                mc = slice(col, col + P)
                nc.tensor.matmul_mx(
                    out=accs[m][:],
                    lhsT=wh_codes[:, c, mc].bitcast(FP8X4),
                    lhsT_scale=wh_scales[:, c, mc],
                    rhs=h_codes[:, c, :].bitcast(FP8X4),
                    rhs_scale=h_scales[:, c, :],
                    start=(c == 0),
                    stop=(c == 3),
                )

        def drain_g(m, on_vector):
            g, t4 = divmod(m, 4)
            if t4 == 0:
                gp[g] = gpp.tile([P, 4, B], BF16, name="gp%d" % g, tag="gp")
            if on_vector:
                nc.vector.tensor_scalar(
                    out=gp[g][:, t4, :],
                    in0=accs[m][:],
                    scalar1=bias[:, m : m + 1],
                    scalar2=0.0,
                    op0=ALU.add,
                    op1=ALU.max,
                )
            else:
                nc.scalar.activation(
                    out=gp[g][:, t4, :], in_=accs[m][:], func=ACT.Relu, bias=bias[:, m : m + 1], scale=1.0
                )

        def regroup_g(g):
            gg[g] = grp.tile([P, 4 * B], BF16, name="gg%d" % g, tag="grp", align_bytes=64)
            regroup(nc.vector.tensor_copy, gg[g][:], gp[g][:])

        def quantise_g(g):
            nc.vector.quantize_mx(
                out=g_codes[:, g, :].bitcast(FP8X4), scales=g_scales[:, g, :], in_=gg[g][:]
            )

        def regroup_wo(q):
            st = stagep.tile([P, 4 * HALF], BF16, name="sq%d" % q, tag="stage", align_bytes=64)
            stage[8 + q] = st
            for g in range(4):
                eng = nc.vector.tensor_copy if g < WO_V_PASSES[q] else nc.scalar.copy
                piece = raw[8 + 2 * (q // 2) + g // 2][:].rearrange("p a (b n) -> p (a b) n", b=2)
                rows = slice(4 * (g % 2), 4 * (g % 2) + 4)
                cols = slice(256 * (q % 2), 256 * (q % 2) + 256)
                regroup(eng, st[:, HALF * g : HALF * g + HALF], piece[:, rows, cols])

        def quantise_wo(q):
            nc.vector.quantize_mx(
                out=wo_codes[:, q, :].bitcast(FP8X4), scales=wo_scales[:, q, :], in_=stage[8 + q][:]
            )

        banks = {}

        def x_plus_bias(q):
            for hb in range(2):
                xb = ps.tile([P, 512], F32, name="xb%d_%d" % (q, hb), tag="bank")
                for k in range(2):
                    cols = slice(256 * k, 256 * k + 256)
                    nc.tensor.matmul(
                        out=xb[:, cols],
                        lhsT=ident_bf[:],
                        rhs=x_sb[2 * hb + k][:].rearrange("p (j e) -> p e j", e=2)[:, 0, 256 * q : 256 * q + 256],
                        start=True,
                        stop=False,
                    )
                    nc.tensor.matmul(
                        out=xb[:, cols],
                        lhsT=ones_bf[:],
                        rhs=brow[:, 256 * q : 256 * q + 256],
                        start=False,
                        stop=True,
                    )
                nc.scalar.copy(out=tplane[q % 2][:, 0, 512 * hb : 512 * hb + 512], in_=xb[:])

        def x_odd(u):
            q = u // 2
            for bt in (2 * (u % 2), 2 * (u % 2) + 1):
                banks[(q, bt)] = ps.tile([P, 512], F32, name="sh%d_%d" % (q, bt), tag="bank")
                nc.tensor.matmul(
                    out=banks[(q, bt)][:, 256:512],
                    lhsT=ident_bf[:],
                    rhs=x_sb[bt][:].rearrange("p (j e) -> p e j", e=2)[:, 1, 256 * q : 256 * q + 256],
                    start=True,
                    stop=True,
                )

        def matmul2(q, bt):
            for g in range(4):
                nc.tensor.matmul_mx(
                    out=banks[(q, bt)][:, 0:256],
                    lhsT=g_codes[:, g, P * bt : P * bt + P].bitcast(FP8X4),
                    lhsT_scale=g_scales[:, g, P * bt : P * bt + P],
                    rhs=wo_codes[:, q, 256 * g : 256 * g + 256].bitcast(FP8X4),
                    rhs_scale=wo_scales[:, q, 256 * g : 256 * g + 256],
                    start=(g == 0),
                    stop=(g == 3),
                )

        def add_and_store(q, bt):
            o = outp.tile([P, 512], F32, name="o%d_%d" % (q, bt), tag="o")
            nc.vector.tensor_tensor(
                out=o[:].rearrange("p (k i e) -> p k e i", i=2, e=2),
                in0=banks[(q, bt)][:].rearrange("p (e k i) -> p k e i", e=2, i=2),
                in1=tplane[q % 2][:, :, 256 * bt : 256 * bt + 256].rearrange("p e (k i) -> p k e i", i=2),
                op=ALU.add,
            )
            nc.sync.dma_start(out=out[P * bt : P * bt + P, 512 * q : 512 * q + 512], in_=o[:])

        warm = const.tile([P, 2], F32, name="warm")
        nc.vector.memset(warm[:, 0:1], 0.0)
        nc.scalar.activation(out=warm[:, 1:2], in_=warm[:, 0:1], func=ACT.Relu)

        load_raw(0)
        load_raw(1)
        for bt in range(4):
            t = act.tile([P, MID], BF16, name="h%d" % bt, tag="act")
            nc.sync.dma_start(out=t[:], in_=h[P * bt : P * bt + P, :])
            h_sb.append(t)
        for i in range(2, RAW_BUFS):
            load_raw(i)

        ident = const.tile([P, P], F32, name="ident")
        make_identity(nc, ident[:])
        ident_bf = const.tile([P, P], BF16, name="ident_bf")
        make_identity(nc, ident_bf[:])
        ones_bf = const.tile([P, P], BF16, name="ones_bf")
        nc.vector.memset(ones_bf[:], 1.0)
        brow = const.tile([P, HALF], BF16, name="brow")
        nc.vector.memset(brow[:], 0.0)
        nc.scalar.dma_start(out=brow[0:1, :], in_=b_out.rearrange("(o n) -> o n", o=1))
        tplane = []
        for k in range(2):
            tpl = const.tile([P, 2, HALF], F32, name="tplane%d" % k)
            nc.vector.memset(tpl[:, 1, :], 0.0)
            tplane.append(tpl)
        bias = const.tile([P, 16], BF16, name="bias")
        nc.scalar.dma_start(
            out=bias[:].rearrange("p (g t) -> p g t", t=4), in_=b_h.rearrange("(g p t) -> p g t", p=P, t=4)
        )

        regroup_wh(0)
        quantise_wh(0)
        regroup_wh(1)
        quantise_wh(1)

        gh = []
        for c in range(4):
            gh.append(grp.tile([P, 4 * B], BF16, name="gh%d" % c, tag="grp", align_bytes=64))
        for bh in range(2):
            for c in range(4):
                tp = ps.tile([P, 512], F32, name="tp%d_%d" % (bh, c), tag="bank")
                for u in range(2):
                    for b2 in range(2):
                        words = h_sb[2 * bh + b2][:].bitcast(F32).rearrange(
                            "p (c q u) -> p c u q", c=4, u=2
                        )
                        nc.tensor.transpose(
                            out=tp[:, 256 * u + P * b2 : 256 * u + P * b2 + P],
                            in_=words[:, c, u, :],
                            identity=ident[:],
                        )
                dst = gh[c][:].bitcast(F32).rearrange("p (b u) -> p b u", u=2)
                nc.scalar.copy(
                    out=dst[:, 256 * bh : 256 * bh + 256, :], in_=tp[:].rearrange("p (u b) -> p b u", u=2)
                )
        for c in range(4):
            nc.vector.quantize_mx(
                out=h_codes[:, c, :].bitcast(FP8X4), scales=h_scales[:, c, :], in_=gh[c][:]
            )
        matmul1(0)
        matmul1(1)

        regroup_wh(2)
        for i in range(2, 8):
            if i + 1 < 8:
                regroup_wh(i + 1)
            quantise_wh(i)
            if i == 3:
                for bt in range(4):
                    t = act.tile([P, MID], BF16, name="x%d" % bt, tag="act")
                    nc.sync.dma_start(out=t[:], in_=x[P * bt : P * bt + P, :])
                    x_sb.append(t)
            matmul1(i)
            if i == 4:
                for m in range(8):
                    drain_g(m, False)
            if i == 5:
                regroup_g(0)
                quantise_g(0)
            if i == 6:
                regroup_g(1)
                quantise_g(1)
        regroup_wo(0)
        quantise_wo(0)
        for m in range(8, 16):
            drain_g(m, m in (9, 11))
            if m == 11:
                regroup_g(2)
        quantise_g(2)
        regroup_g(3)
        quantise_g(3)
        regroup_wo(1)
        quantise_wo(1)

        x_plus_bias(0)
        x_odd(0)
        x_odd(1)
        for u in range(8):
            q, second = divmod(u, 2)
            pair = (2 * second, 2 * second + 1)
            for bt in pair:
                matmul2(q, bt)
            if second == 0 and q + 1 < 4:
                x_plus_bias(q + 1)
            if u + 2 < 8:
                x_odd(u + 2)
            if q + 2 < 4:
                if second == 0:
                    regroup_wo(q + 2)
                else:
                    quantise_wo(q + 2)
            for bt in pair:
                add_and_store(q, bt)
